import numpy as np
import ml_dtypes


def mxq(x, axis, fmt="e4m3"):
    dtype, down = {"e4m3": (ml_dtypes.float8_e4m3fn, 7), "e5m2": (ml_dtypes.float8_e5m2, 14)}[fmt]
    v = np.moveaxis(np.asarray(x, np.float32).astype(ml_dtypes.bfloat16).astype(np.float64), axis, -1)
    blocks = v.reshape(v.shape[:-1] + (-1, 32))
    amax = np.abs(blocks).max(-1, keepdims=True)
    byte = np.maximum(np.where(amax > 0, np.frexp(amax)[1] - 1 + 127, 0) - down, 1)
    scale = np.exp2(byte - 127.0)
    codes = (blocks / scale).astype(np.float32).astype(dtype).astype(np.float64)
    return np.moveaxis((codes * scale).reshape(v.shape), -1, axis)


WIDE = False


def mx_kscale(k):
    if not WIDE:
        return np.ones(k)
    levels = np.array([10, -10, 5, -5, 0])
    if k % 512:
        return np.exp2(np.random.permutation(np.resize(levels, k // 32))).repeat(32)
    a = np.empty((k // 512, 16))
    for p in range(k // 512):
        a[p, :8] = np.random.permutation(np.resize(levels, 8))
        for g in range(8):
            far = levels[np.abs(levels - a[p, g]) >= 10]
            a[p, g + 8] = far[np.random.randint(len(far))]
    return np.exp2(a.ravel()).repeat(32)


BF16 = ml_dtypes.bfloat16


def bf(x):
    return np.asarray(x, np.float32).astype(BF16)


def f64(x):
    return np.asarray(x).astype(np.float64)


B, L, H, D = 16, 256, 4, 128
DIM = H * D


def setup_inputs():
    r = np.random.standard_normal
    s = mx_kscale(DIM)
    ang = np.arange(L)[:, None, None] * (r((H, D)) * 0.2)[None]
    return {"x": bf(r((B, L, DIM)) * s),
            "wq_w": bf(r((DIM, DIM)) * 0.5 / np.sqrt(DIM) / s[None, :]),
            "wq_b": bf(r(DIM) * 0.1),
            "wk_w": bf(r((DIM, DIM)) * 0.5 / np.sqrt(DIM) / s[None, :]),
            "wk_b": bf(r(DIM) * 0.1),
            "rot_re": bf(np.cos(ang)),
            "rot_im": bf(np.sin(ang))}


def reference(x, wq_w, wq_b, wk_w, wk_b, rot_re, rot_im):
    xq = mxq(f64(x), 2, "e4m3")
    q = ((xq @ mxq(f64(wq_w), 1, "e4m3").T) + f64(wq_b)).reshape(B, L, H, D)
    k = ((xq @ mxq(f64(wk_w), 1, "e4m3").T) + f64(wk_b)).reshape(B, L, H, D)
    c = f64(rot_re)[None]
    sn = f64(rot_im)[None]
    return q * c, q * sn, k * c, -(k * sn)

@@ -1,0 +1,228 @@
+import concourse.mybir as mybir
+from concourse.masks import make_identity
+
+F32 = mybir.dt.float32
+BF16 = mybir.dt.bfloat16
+U32 = mybir.dt.uint32
+U8 = mybir.dt.uint8
+FP8X4 = mybir.dt.float8_e4m3fn_x4
+MULT = mybir.AluOpType.mult
+IDENTITY = mybir.ActivationFunctionType.Identity
+
+P = 128
+DIM = 512
+TOKENS = 16 * 256
+POSITIONS = 256
+SUBS = 4
+ROWS = P * SUBS
+GROUPS = TOKENS // ROWS
+WORDS = DIM // 2
+HALF = ROWS // 2
+GPSIMD_SUB = 3
+
+FLOPS = 2 * TOKENS * DIM * (2 * DIM)
+
+
+def tile_retention_pa_t_kernel(
+    tc, x, wq_w, wq_b, wk_w, wk_b, rot_re, rot_im, out_0, out_1, out_2, out_3
+):
+    nc = tc.nc
+
+    x_rows = x.rearrange("b l k -> (b l) k")
+    outs = [
+        o.rearrange("b l h d -> (b l) (h d)").rearrange(
+            "(g p i) c -> g p (i c)", p=P, i=SUBS
+        )
+        for o in (out_0, out_1, out_2, out_3)
+    ]
+
+    with tc.manual_schedule(), tc.tile_pool(name="keep", bufs=1) as keep, tc.tile_pool(
+        name="x_in", bufs=GROUPS
+    ) as x_in, tc.tile_pool(name="stage", bufs=2) as stage, tc.tile_pool(
+        name="results", bufs=6
+    ) as results, tc.psum_pool(name="psum_words", bufs=2) as psum_words, tc.psum_pool(
+        name="psum_acc", bufs=2
+    ) as psum_acc, tc.psum_pool(name="psum_back", bufs=4) as psum_back:
+        bias_rows = keep.tile([P, P], BF16)
+        nc.vector.memset(bias_rows[:], 0.0)
+        nc.scalar.dma_start(
+            out=bias_rows[0:SUBS, :], in_=wq_b.rearrange("(m c) -> m c", c=P)
+        )
+        nc.scalar.dma_start(
+            out=bias_rows[SUBS : 2 * SUBS, :], in_=wk_b.rearrange("(m c) -> m c", c=P)
+        )
+        rot_table = keep.tile([P, 3, SUBS, DIM], BF16)
+        for plane, rot in ((0, rot_im), (1, rot_re)):
+            rot_rows = rot.rearrange("l h d -> l (h d)").rearrange(
+                "(p i) c -> p i c", i=SUBS
+            )
+            for first in (0, POSITIONS // SUBS):
+                nc.scalar.dma_start(
+                    out=rot_table[first : first + POSITIONS // SUBS, plane, :, :],
+                    in_=rot_rows,
+                )
+
+        warm = keep.tile([P, 2], F32)
+        nc.vector.memset(warm[:], 0.0)
+        nc.scalar.activation(out=warm[:, 1:2], in_=warm[:, 0:1], func=IDENTITY)
+
+        w_raw = {}
+        x_raw = {}
+
+        def load_weight(name, w):
+            w_raw[name] = keep.tile([P, SUBS * DIM], BF16, name="w_raw_" + name)
+            nc.sync.dma_start(
+                out=w_raw[name][:].rearrange("p (m k) -> p m k", m=SUBS),
+                in_=w.rearrange("(m p) k -> p m k", p=P),
+            )
+
+        def load_tokens(g):
+            x_raw[g] = x_in.tile([P, SUBS * DIM], BF16, name="x_raw", tag="x_raw")
+            nc.sync.dma_start(
+                out=x_raw[g][:],
+                in_=x_rows[g * ROWS : (g + 1) * ROWS, :].rearrange(
+                    "(p i) k -> p (i k)", i=SUBS
+                ),
+            )
+
+        load_weight("q", wq_w)
+        load_tokens(0)
+        load_weight("k", wk_w)
+        for g in range(1, GROUPS):
+            load_tokens(g)
+
+        ident = keep.tile([P, P], F32)
+        make_identity(nc, ident[:])
+
+        def transpose_words(raw, copy_first_half):
+            grouped = stage.tile([P, ROWS * 4], BF16, name="grouped", align_bytes=64)
+            grouped_words = grouped[:].bitcast(F32).rearrange("p (r u) -> p r u", u=2)
+            raw_words = raw[:].bitcast(F32)
+            for half in range(2):
+                words_t = psum_words.tile([P, 2, HALF], F32, name="words_t")
+                for j in range(2):
+                    sub = 2 * half + j
+                    for u in range(2):
+                        nc.tensor.transpose(
+                            words_t[:, u, j * P : (j + 1) * P],
+                            raw_words[:, sub * WORDS + u : (sub + 1) * WORDS : 2],
+                            ident[:],
+                        )
+                copy_out = copy_first_half if half == 0 else nc.scalar.copy
+                copy_out(
+                    out=grouped_words[:, half * HALF : (half + 1) * HALF, :],
+                    in_=words_t[:].rearrange("p u r -> p r u"),
+                )
+            return grouped
+
+        def quantise(grouped, codes, scales):
+            nc.vector.quantize_mx(
+                out=codes[:].bitcast(FP8X4), scales=scales[:], in_=grouped[:]
+            )
+
+        def project(name, bias_first, x_codes, x_scales):
+            projected = stage.tile([P, SUBS, ROWS], F32, name="projected")
+            for m in range(SUBS):
+                acc = psum_acc.tile([P, ROWS], F32, name="acc")
+                nc.tensor.matmul_mx(
+                    out=acc[:],
+                    lhsT=w_codes[name][:, m * P : (m + 1) * P].bitcast(FP8X4),
+                    lhsT_scale=w_scales[name][:, m * P : (m + 1) * P],
+                    rhs=x_codes[:].bitcast(FP8X4),
+                    rhs_scale=x_scales[:],
+                    start=True,
+                    stop=True,
+                )
+                nc.scalar.activation(
+                    out=projected[:, m, :],
+                    in_=acc[:],
+                    func=IDENTITY,
+                    bias=bias_cols[:, bias_first + m : bias_first + m + 1],
+                    scale=1.0,
+                )
+            return projected
+
+        def rotate_and_store(g, projected, first_plane, pair_outs, store_pieces):
+            rotated = results.tile([P, 2, SUBS, DIM], F32, name="rotated")
+            subs_a_piece = SUBS // store_pieces
+            for i in range(SUBS):
+                back = psum_back.tile([P, DIM], F32, name="back")
+                for m in range(SUBS):
+                    nc.tensor.transpose(
+                        back[:, m * P : (m + 1) * P],
+                        projected[:, m, i * P : (i + 1) * P],
+                        ident[:],
+                    )
+                planes = rot_table[:, first_plane : first_plane + 2, i, :]
+                if i == GPSIMD_SUB:
+                    back_sb = stage.tile([P, DIM], F32, name="back_sb")
+                    nc.scalar.copy(out=back_sb[:], in_=back[:])
+                    nc.gpsimd.tensor_tensor(
+                        out=rotated[:, :, i, :],
+                        in0=back_sb[:].unsqueeze(1).to_broadcast([P, 2, DIM]),
+                        in1=planes,
+                        op=MULT,
+                    )
+                else:
+                    nc.vector.tensor_tensor(
+                        out=rotated[:, :, i, :],
+                        in0=back[:].unsqueeze(1).to_broadcast([P, 2, DIM]),
+                        in1=planes,
+                        op=MULT,
+                    )
+                if (i + 1) % subs_a_piece == 0:
+                    piece_start = i + 1 - subs_a_piece
+                    for slot in range(2):
+                        nc.sync.dma_start(
+                            out=pair_outs[slot][g][:, piece_start * DIM : (i + 1) * DIM],
+                            in_=rotated[:, slot, piece_start : i + 1, :].rearrange(
+                                "p i c -> p (i c)"
+                            ),
+                        )
+
+        w_codes = {}
+        w_scales = {}
+        for name in ("q", "k"):
+            w_codes[name] = keep.tile([P, ROWS], U32, name="w_codes_" + name, align_bytes=64)
+            w_scales[name] = keep.tile([P, ROWS], U8, name="w_scales_" + name, align_bytes=64)
+
+        x_codes = {}
+        x_scales = {}
+
+        def quantise_tokens(g, grouped):
+            x_codes[g] = stage.tile([P, ROWS], U32, name="x_codes", align_bytes=64)
+            x_scales[g] = stage.tile([P, ROWS], U8, name="x_scales", align_bytes=64)
+            quantise(grouped, x_codes[g], x_scales[g])
+
+        grouped_wq = transpose_words(w_raw["q"], nc.vector.tensor_copy)
+        grouped_x = {0: transpose_words(x_raw[0], nc.vector.tensor_copy)}
+
+        bias_rows_f32 = keep.tile([P, P], F32)
+        nc.vector.tensor_copy(out=bias_rows_f32[:], in_=bias_rows[:])
+        bias_t = psum_words.tile([P, 2, HALF], F32, name="words_t")
+        nc.tensor.transpose(bias_t[:, 0, 0:P], bias_rows_f32[:], ident[:])
+        quantise(grouped_wq, w_codes["q"], w_scales["q"])
+        bias_cols = keep.tile([P, 2 * SUBS], F32)
+        nc.vector.tensor_copy(out=bias_cols[:], in_=bias_t[:, 0, 0 : 2 * SUBS])
+        quantise_tokens(0, grouped_x[0])
+
+        grouped_wk = transpose_words(w_raw["k"], nc.vector.tensor_copy)
+        projected_q = project("q", 0, x_codes[0], x_scales[0])
+        quantise(grouped_wk, w_codes["k"], w_scales["k"])
+        grouped_x[1] = transpose_words(x_raw[1], nc.vector.tensor_copy)
+        nc.vector.tensor_scalar_mul(
+            out=rot_table[:, 2, :, :], in0=rot_table[:, 0, :, :], scalar1=-1.0
+        )
+
+        for g in range(GROUPS):
+            if g + 1 < GROUPS:
+                quantise_tokens(g + 1, grouped_x[g + 1])
+            projected_k = project("k", SUBS, x_codes[g], x_scales[g])
+            rotate_and_store(
+                g, projected_q, 0, (outs[1], outs[0]), SUBS if g == 0 else 1
+            )
+            if g + 1 < GROUPS:
+                projected_q = project("q", 0, x_codes[g + 1], x_scales[g + 1])
+            if g + 2 < GROUPS:
+                grouped_x[g + 2] = transpose_words(x_raw[g + 2], nc.scalar.copy)
+            rotate_and_store(g, projected_k, 1, (outs[2], outs[3]), 1)

@@ -12,10 +12,10 @@ IDENTITY = mybir.ActivationFunctionType.Identity
 P = 128
 DIM = 512
 TOKENS = 16 * 256
-POSITIONS = 256
 SUBS = 4
 ROWS = P * SUBS
 GROUPS = TOKENS // ROWS
+PAIR = 2
 WORDS = DIM // 2
 HALF = ROWS // 2
 GPSIMD_SUB = 3
@@ -43,6 +43,8 @@ def tile_retention_pa_t_kernel(
     ) as results, tc.psum_pool(name="psum_words", bufs=2) as psum_words, tc.psum_pool(
         name="psum_acc", bufs=2
     ) as psum_acc, tc.psum_pool(name="psum_back", bufs=4) as psum_back:
+        ident = keep.tile([P, P], F32)
+        make_identity(nc, ident[:])
         bias_rows = keep.tile([P, P], BF16)
         nc.vector.memset(bias_rows[:], 0.0)
         nc.scalar.dma_start(
@@ -52,15 +54,6 @@ def tile_retention_pa_t_kernel(
             out=bias_rows[SUBS : 2 * SUBS, :], in_=wk_b.rearrange("(m c) -> m c", c=P)
         )
         rot_table = keep.tile([P, 3, SUBS, DIM], BF16)
-        for plane, rot in ((0, rot_im), (1, rot_re)):
-            rot_rows = rot.rearrange("l h d -> l (h d)").rearrange(
-                "(p i) c -> p i c", i=SUBS
-            )
-            for first in (0, POSITIONS // SUBS):
-                nc.scalar.dma_start(
-                    out=rot_table[first : first + POSITIONS // SUBS, plane, :, :],
-                    in_=rot_rows,
-                )
 
         warm = keep.tile([P, 2], F32)
         nc.vector.memset(warm[:], 0.0)
@@ -87,12 +80,26 @@ def tile_retention_pa_t_kernel(
 
         load_weight("q", wq_w)
         load_tokens(0)
+        rot_raw = keep.tile([P, 2, PAIR, DIM], BF16)
+        for plane, rot in ((0, rot_im), (1, rot_re)):
+            nc.sync.dma_start(
+                out=rot_raw[:, plane, :, :].rearrange("p s c -> p (s c)"),
+                in_=rot.rearrange("(p s) h d -> p (s h d)", s=PAIR),
+            )
         load_weight("k", wk_w)
         for g in range(1, GROUPS):
             load_tokens(g)
 
-        ident = keep.tile([P, P], F32)
-        make_identity(nc, ident[:])
+        ident_bf16 = keep.tile([P, P], BF16)
+        nc.vector.tensor_copy(out=ident_bf16[:], in_=ident[:])
+        pick = keep.tile([P, PAIR, P], BF16)
+        nc.vector.tensor_copy(
+            out=pick[:].rearrange("p h (r q) -> p h r q", r=PAIR),
+            in_=ident_bf16[:]
+            .rearrange("p (q h) -> p h q", h=PAIR)
+            .unsqueeze(2)
+            .to_broadcast([P, PAIR, PAIR, P // PAIR]),
+        )
 
         def transpose_words(raw, copy_first_half):
             grouped = stage.tile([P, ROWS * 4], BF16, name="grouped", align_bytes=64)
@@ -146,7 +153,7 @@ def tile_retention_pa_t_kernel(
             rotated = results.tile([P, 2, SUBS, DIM], F32, name="rotated")
             subs_a_piece = SUBS // store_pieces
             for i in range(SUBS):
-                back = psum_back.tile([P, DIM], F32, name="back")
+                back = psum_back.tile([P, DIM], F32, name="back", tag="back")
                 for m in range(SUBS):
                     nc.tensor.transpose(
                         back[:, m * P : (m + 1) * P],
@@ -180,6 +187,18 @@ def tile_retention_pa_t_kernel(
                             ),
                         )
 
+        def spread_rotation(i):
+            spread = psum_back.tile([P, 2, DIM], BF16, name="spread", tag="back")
+            for plane in range(2):
+                nc.tensor.matmul(
+                    spread[:, plane, :],
+                    lhsT=pick[:, i // PAIR, :],
+                    rhs=rot_raw[:, plane, i % PAIR, :],
+                    start=True,
+                    stop=True,
+                )
+            nc.vector.tensor_copy(out=rot_table[:, 0:2, i, :], in_=spread[:])
+
         w_codes = {}
         w_scales = {}
         for name in ("q", "k"):
@@ -205,9 +224,13 @@ def tile_retention_pa_t_kernel(
         bias_cols = keep.tile([P, 2 * SUBS], F32)
         nc.vector.tensor_copy(out=bias_cols[:], in_=bias_t[:, 0, 0 : 2 * SUBS])
         quantise_tokens(0, grouped_x[0])
+        spread_rotation(0)
+        spread_rotation(1)
 
         grouped_wk = transpose_words(w_raw["k"], nc.vector.tensor_copy)
         projected_q = project("q", 0, x_codes[0], x_scales[0])
+        spread_rotation(2)
+        spread_rotation(3)
         quantise(grouped_wk, w_codes["k"], w_scales["k"])
         grouped_x[1] = transpose_words(x_raw[1], nc.vector.tensor_copy)
         nc.vector.tensor_scalar_mul(
@@ -218,11 +241,10 @@ def tile_retention_pa_t_kernel(
             if g + 1 < GROUPS:
                 quantise_tokens(g + 1, grouped_x[g + 1])
             projected_k = project("k", SUBS, x_codes[g], x_scales[g])
-            rotate_and_store(
-                g, projected_q, 0, (outs[1], outs[0]), SUBS if g == 0 else 1
-            )
+            pieces = SUBS if g == 0 else 1
+            rotate_and_store(g, projected_q, 0, (outs[1], outs[0]), pieces)
             if g + 1 < GROUPS:
                 projected_q = project("q", 0, x_codes[g + 1], x_scales[g + 1])
             if g + 2 < GROUPS:
                 grouped_x[g + 2] = transpose_words(x_raw[g + 2], nc.scalar.copy)
-            rotate_and_store(g, projected_k, 1, (outs[2], outs[3]), 1)
+            rotate_and_store(g, projected_k, 1, (outs[2], outs[3]), pieces)

@@ -18,7 +18,9 @@ GROUPS = TOKENS // ROWS
 PAIR = 2
 WORDS = DIM // 2
 HALF = ROWS // 2
-GPSIMD_SUB = 3
+GPSIMD_SUB = 1
+FIRST_BIAS = {"q": 0, "k": SUBS}
+FIRST_PLANE = {"q": 0, "k": 1}
 
 FLOPS = 2 * TOKENS * DIM * (2 * DIM)
 
@@ -101,25 +103,30 @@ def tile_retention_pa_t_kernel(
             .to_broadcast([P, PAIR, PAIR, P // PAIR]),
         )
 
-        def transpose_words(raw, copy_first_half):
-            grouped = stage.tile([P, ROWS * 4], BF16, name="grouped", align_bytes=64)
+        def transpose_half(raw, grouped, half, copy_out):
             grouped_words = grouped[:].bitcast(F32).rearrange("p (r u) -> p r u", u=2)
             raw_words = raw[:].bitcast(F32)
-            for half in range(2):
-                words_t = psum_words.tile([P, 2, HALF], F32, name="words_t")
-                for j in range(2):
-                    sub = 2 * half + j
-                    for u in range(2):
-                        nc.tensor.transpose(
-                            words_t[:, u, j * P : (j + 1) * P],
-                            raw_words[:, sub * WORDS + u : (sub + 1) * WORDS : 2],
-                            ident[:],
-                        )
-                copy_out = copy_first_half if half == 0 else nc.scalar.copy
-                copy_out(
-                    out=grouped_words[:, half * HALF : (half + 1) * HALF, :],
-                    in_=words_t[:].rearrange("p u r -> p r u"),
-                )
+            words_t = psum_words.tile([P, 2, HALF], F32, name="words_t")
+            for j in range(2):
+                sub = 2 * half + j
+                for u in range(2):
+                    nc.tensor.transpose(
+                        words_t[:, u, j * P : (j + 1) * P],
+                        raw_words[:, sub * WORDS + u : (sub + 1) * WORDS : 2],
+                        ident[:],
+                    )
+            copy_out(
+                out=grouped_words[:, half * HALF : (half + 1) * HALF, :],
+                in_=words_t[:].rearrange("p u r -> p r u"),
+            )
+
+        def new_grouped():
+            return stage.tile([P, ROWS * 4], BF16, name="grouped", align_bytes=64)
+
+        def transpose_words(raw):
+            grouped = new_grouped()
+            transpose_half(raw, grouped, 0, nc.vector.tensor_copy)
+            transpose_half(raw, grouped, 1, nc.scalar.copy)
             return grouped
 
         def quantise(grouped, codes, scales):
@@ -127,65 +134,61 @@ def tile_retention_pa_t_kernel(
                 out=codes[:].bitcast(FP8X4), scales=scales[:], in_=grouped[:]
             )
 
-        def project(name, bias_first, x_codes, x_scales):
-            projected = stage.tile([P, SUBS, ROWS], F32, name="projected")
-            for m in range(SUBS):
-                acc = psum_acc.tile([P, ROWS], F32, name="acc")
-                nc.tensor.matmul_mx(
-                    out=acc[:],
-                    lhsT=w_codes[name][:, m * P : (m + 1) * P].bitcast(FP8X4),
-                    lhsT_scale=w_scales[name][:, m * P : (m + 1) * P],
-                    rhs=x_codes[:].bitcast(FP8X4),
-                    rhs_scale=x_scales[:],
-                    start=True,
-                    stop=True,
-                )
-                nc.scalar.activation(
-                    out=projected[:, m, :],
-                    in_=acc[:],
-                    func=IDENTITY,
-                    bias=bias_cols[:, bias_first + m : bias_first + m + 1],
-                    scale=1.0,
-                )
-            return projected
+        def new_projected():
+            return stage.tile([P, SUBS, ROWS], F32, name="projected")
 
-        def rotate_and_store(g, projected, first_plane, pair_outs, store_pieces):
-            rotated = results.tile([P, 2, SUBS, DIM], F32, name="rotated")
-            subs_a_piece = SUBS // store_pieces
-            for i in range(SUBS):
-                back = psum_back.tile([P, DIM], F32, name="back", tag="back")
-                for m in range(SUBS):
-                    nc.tensor.transpose(
-                        back[:, m * P : (m + 1) * P],
-                        projected[:, m, i * P : (i + 1) * P],
-                        ident[:],
-                    )
-                planes = rot_table[:, first_plane : first_plane + 2, i, :]
-                if i == GPSIMD_SUB:
-                    back_sb = stage.tile([P, DIM], F32, name="back_sb")
-                    nc.scalar.copy(out=back_sb[:], in_=back[:])
-                    nc.gpsimd.tensor_tensor(
-                        out=rotated[:, :, i, :],
-                        in0=back_sb[:].unsqueeze(1).to_broadcast([P, 2, DIM]),
-                        in1=planes,
-                        op=MULT,
-                    )
-                else:
-                    nc.vector.tensor_tensor(
-                        out=rotated[:, :, i, :],
-                        in0=back[:].unsqueeze(1).to_broadcast([P, 2, DIM]),
-                        in1=planes,
-                        op=MULT,
-                    )
-                if (i + 1) % subs_a_piece == 0:
-                    piece_start = i + 1 - subs_a_piece
-                    for slot in range(2):
-                        nc.sync.dma_start(
-                            out=pair_outs[slot][g][:, piece_start * DIM : (i + 1) * DIM],
-                            in_=rotated[:, slot, piece_start : i + 1, :].rearrange(
-                                "p i c -> p (i c)"
-                            ),
-                        )
+        def project(g, name, projected, m):
+            bias = FIRST_BIAS[name] + m
+            acc = psum_acc.tile([P, ROWS], F32, name="acc")
+            nc.tensor.matmul_mx(
+                out=acc[:],
+                lhsT=w_codes[name][:, m * P : (m + 1) * P].bitcast(FP8X4),
+                lhsT_scale=w_scales[name][:, m * P : (m + 1) * P],
+                rhs=x_codes[g][:].bitcast(FP8X4),
+                rhs_scale=x_scales[g][:],
+                start=True,
+                stop=True,
+            )
+            nc.scalar.activation(
+                out=projected[:, m, :],
+                in_=acc[:],
+                func=IDENTITY,
+                bias=bias_cols[:, bias : bias + 1],
+                scale=1.0,
+            )
+
+        def rotate(name, projected, rotated, i):
+            back = psum_back.tile([P, DIM], F32, name="back", tag="back")
+            for m in range(SUBS):
+                nc.tensor.transpose(
+                    back[:, m * P : (m + 1) * P],
+                    projected[:, m, i * P : (i + 1) * P],
+                    ident[:],
+                )
+            planes = rot_table[:, FIRST_PLANE[name] : FIRST_PLANE[name] + 2, i, :]
+            if i == GPSIMD_SUB:
+                back_sb = stage.tile([P, DIM], F32, name="back_sb")
+                nc.scalar.copy(out=back_sb[:], in_=back[:])
+                nc.gpsimd.tensor_tensor(
+                    out=rotated[:, :, i, :],
+                    in0=back_sb[:].unsqueeze(1).to_broadcast([P, 2, DIM]),
+                    in1=planes,
+                    op=MULT,
+                )
+            else:
+                nc.vector.tensor_tensor(
+                    out=rotated[:, :, i, :],
+                    in0=back[:].unsqueeze(1).to_broadcast([P, 2, DIM]),
+                    in1=planes,
+                    op=MULT,
+                )
+
+        def store(g, name, rotated, first, last):
+            for slot in range(2):
+                nc.sync.dma_start(
+                    out=pair_outs[name][slot][g][:, first * DIM : last * DIM],
+                    in_=rotated[:, slot, first:last, :].rearrange("p i c -> p (i c)"),
+                )
 
         def spread_rotation(i):
             spread = psum_back.tile([P, 2, DIM], BF16, name="spread", tag="back")
@@ -198,6 +201,8 @@ def tile_retention_pa_t_kernel(
                     stop=True,
                 )
             nc.vector.tensor_copy(out=rot_table[:, 0:2, i, :], in_=spread[:])
+
+        pair_outs = {"q": (outs[1], outs[0]), "k": (outs[2], outs[3])}
 
         w_codes = {}
         w_scales = {}
@@ -213,8 +218,8 @@ def tile_retention_pa_t_kernel(
             x_scales[g] = stage.tile([P, ROWS], U8, name="x_scales", align_bytes=64)
             quantise(grouped, x_codes[g], x_scales[g])
 
-        grouped_wq = transpose_words(w_raw["q"], nc.vector.tensor_copy)
-        grouped_x = {0: transpose_words(x_raw[0], nc.vector.tensor_copy)}
+        grouped_wq = transpose_words(w_raw["q"])
+        grouped_x = {0: transpose_words(x_raw[0])}
 
         bias_rows_f32 = keep.tile([P, P], F32)
         nc.vector.tensor_copy(out=bias_rows_f32[:], in_=bias_rows[:])
@@ -227,24 +232,38 @@ def tile_retention_pa_t_kernel(
         spread_rotation(0)
         spread_rotation(1)
 
-        grouped_wk = transpose_words(w_raw["k"], nc.vector.tensor_copy)
-        projected_q = project("q", 0, x_codes[0], x_scales[0])
+        grouped_wk = transpose_words(w_raw["k"])
+        projected = new_projected()
+        for m in range(SUBS):
+            project(0, "q", projected, m)
         spread_rotation(2)
         spread_rotation(3)
         quantise(grouped_wk, w_codes["k"], w_scales["k"])
-        grouped_x[1] = transpose_words(x_raw[1], nc.vector.tensor_copy)
+        grouped_x[1] = transpose_words(x_raw[1])
         nc.vector.tensor_scalar_mul(
             out=rot_table[:, 2, :, :], in0=rot_table[:, 0, :, :], scalar1=-1.0
         )
 
-        for g in range(GROUPS):
-            if g + 1 < GROUPS:
+        steps = [(g, name) for g in range(GROUPS) for name in ("q", "k")]
+        for step, (g, name) in enumerate(steps):
+            if name == "q" and g + 1 < GROUPS:
                 quantise_tokens(g + 1, grouped_x[g + 1])
-            projected_k = project("k", SUBS, x_codes[g], x_scales[g])
-            pieces = SUBS if g == 0 else 1
-            rotate_and_store(g, projected_q, 0, (outs[1], outs[0]), pieces)
-            if g + 1 < GROUPS:
-                projected_q = project("q", 0, x_codes[g + 1], x_scales[g + 1])
+            rotated = results.tile([P, 2, SUBS, DIM], F32, name="rotated")
+            next_projected = new_projected()
+            for first in (0, 2):
+                for m in (first, first + 1):
+                    if step + 1 < len(steps):
+                        project(steps[step + 1][0], steps[step + 1][1], next_projected, m)
+                for i in (first, first + 1):
+                    rotate(name, projected, rotated, i)
+                    if g == 0:
+                        store(g, name, rotated, i, i + 1)
+            if g > 0:
+                store(g, name, rotated, 0, SUBS)
             if g + 2 < GROUPS:
-                grouped_x[g + 2] = transpose_words(x_raw[g + 2], nc.scalar.copy)
-            rotate_and_store(g, projected_k, 1, (outs[2], outs[3]), pieces)
+                if name == "q":
+                    grouped_x[g + 2] = new_grouped()
+                transpose_half(
+                    x_raw[g + 2], grouped_x[g + 2], 0 if name == "q" else 1, nc.scalar.copy
+                )
+            projected = next_projected

@@ -14,11 +14,12 @@ DIM = 512
 TOKENS = 16 * 256
 SUBS = 4
 ROWS = P * SUBS
+HALF = ROWS // 2
 GROUPS = TOKENS // ROWS
 PAIR = 2
 WORDS = DIM // 2
-HALF = ROWS // 2
-GPSIMD_SUB = 1
+GPSIMD_SUB = 3
+BLOCK_PAIRS = ((0, 3), (1, 2))
 FIRST_BIAS = {"q": 0, "k": SUBS}
 FIRST_PLANE = {"q": 0, "k": 1}
 
@@ -31,12 +32,11 @@ def tile_retention_pa_t_kernel(
     nc = tc.nc
 
     x_rows = x.rearrange("b l k -> (b l) k")
-    outs = [
-        o.rearrange("b l h d -> (b l) (h d)").rearrange(
-            "(g p i) c -> g p (i c)", p=P, i=SUBS
-        )
-        for o in (out_0, out_1, out_2, out_3)
-    ]
+    out_rows = [o.rearrange("b l h d -> (b l) (h d)") for o in (out_0, out_1, out_2, out_3)]
+
+    def entry_of(rows, g, b):
+        first = g * ROWS + b * HALF
+        return rows[first : first + HALF, :].rearrange("(p s) c -> p (s c)", s=PAIR)
 
     with tc.manual_schedule(), tc.tile_pool(name="keep", bufs=1) as keep, tc.tile_pool(
         name="x_in", bufs=GROUPS
@@ -45,6 +45,8 @@ def tile_retention_pa_t_kernel(
     ) as results, tc.psum_pool(name="psum_words", bufs=2) as psum_words, tc.psum_pool(
         name="psum_acc", bufs=2
     ) as psum_acc, tc.psum_pool(name="psum_back", bufs=4) as psum_back:
+        zeros = keep.tile([P, DIM], BF16)
+        nc.vector.memset(zeros[:], 0.0)
         ident = keep.tile([P, P], F32)
         make_identity(nc, ident[:])
         bias_rows = keep.tile([P, P], BF16)
@@ -55,58 +57,53 @@ def tile_retention_pa_t_kernel(
         nc.scalar.dma_start(
             out=bias_rows[SUBS : 2 * SUBS, :], in_=wk_b.rearrange("(m c) -> m c", c=P)
         )
-        rot_table = keep.tile([P, 3, SUBS, DIM], BF16)
 
         warm = keep.tile([P, 2], F32)
         nc.vector.memset(warm[:], 0.0)
         nc.scalar.activation(out=warm[:, 1:2], in_=warm[:, 0:1], func=IDENTITY)
 
-        w_raw = {}
-        x_raw = {}
-
-        def load_weight(name, w):
-            w_raw[name] = keep.tile([P, SUBS * DIM], BF16, name="w_raw_" + name)
+        def load_weight(raw, w, first, last):
             nc.sync.dma_start(
-                out=w_raw[name][:].rearrange("p (m k) -> p m k", m=SUBS),
-                in_=w.rearrange("(m p) k -> p m k", p=P),
+                out=raw[:].rearrange("p (m k) -> p m k", m=SUBS)[:, first:last, :],
+                in_=w.rearrange("(m p) k -> p m k", p=P)[:, first:last, :],
             )
 
         def load_tokens(g):
-            x_raw[g] = x_in.tile([P, SUBS * DIM], BF16, name="x_raw", tag="x_raw")
-            nc.sync.dma_start(
-                out=x_raw[g][:],
-                in_=x_rows[g * ROWS : (g + 1) * ROWS, :].rearrange(
-                    "(p i) k -> p (i k)", i=SUBS
-                ),
-            )
+            for b in range(2):
+                nc.sync.dma_start(
+                    out=x_raw[g][:, b * PAIR * DIM : (b + 1) * PAIR * DIM],
+                    in_=entry_of(x_rows, g, b),
+                )
 
-        load_weight("q", wq_w)
+        w_raw = {
+            name: keep.tile([P, SUBS * DIM], BF16, name="w_raw_" + name) for name in ("q", "k")
+        }
+        x_raw = [
+            x_in.tile([P, SUBS * DIM], BF16, name="x_raw", tag="x_raw") for g in range(GROUPS)
+        ]
+        load_weight(w_raw["q"], wq_w, 0, 2)
+        load_weight(w_raw["q"], wq_w, 2, 4)
         load_tokens(0)
-        rot_raw = keep.tile([P, 2, PAIR, DIM], BF16)
+        rot_table = keep.tile([P, 3, PAIR, DIM], BF16)
         for plane, rot in ((0, rot_im), (1, rot_re)):
             nc.sync.dma_start(
-                out=rot_raw[:, plane, :, :].rearrange("p s c -> p (s c)"),
-                in_=rot.rearrange("(p s) h d -> p (s h d)", s=PAIR),
+                out=rot_table[:, plane, :, :].rearrange("p s c -> p (s c)"),
+                in_=rot.rearrange("(p t) h d -> p (t h d)", t=PAIR),
             )
-        load_weight("k", wk_w)
+        load_weight(w_raw["k"], wk_w, 0, 4)
         for g in range(1, GROUPS):
             load_tokens(g)
 
-        ident_bf16 = keep.tile([P, P], BF16)
-        nc.vector.tensor_copy(out=ident_bf16[:], in_=ident[:])
-        pick = keep.tile([P, PAIR, P], BF16)
-        nc.vector.tensor_copy(
-            out=pick[:].rearrange("p h (r q) -> p h r q", r=PAIR),
-            in_=ident_bf16[:]
-            .rearrange("p (q h) -> p h q", h=PAIR)
-            .unsqueeze(2)
-            .to_broadcast([P, PAIR, PAIR, P // PAIR]),
-        )
+        def keep_clock(bank, count):
+            for n in range(count):
+                nc.tensor.matmul(bank, lhsT=zeros[:, 0:P], rhs=zeros[:], start=True, stop=True)
 
-        def transpose_half(raw, grouped, half, copy_out):
+        def transpose_half(raw, grouped, half, copy_out, new_bank, clock=0):
             grouped_words = grouped[:].bitcast(F32).rearrange("p (r u) -> p r u", u=2)
             raw_words = raw[:].bitcast(F32)
-            words_t = psum_words.tile([P, 2, HALF], F32, name="words_t")
+            bank = new_bank()
+            keep_clock(bank[:], clock)
+            words_t = bank[:].rearrange("p (u r) -> p u r", u=2)
             for j in range(2):
                 sub = 2 * half + j
                 for u in range(2):
@@ -117,56 +114,66 @@ def tile_retention_pa_t_kernel(
                     )
             copy_out(
                 out=grouped_words[:, half * HALF : (half + 1) * HALF, :],
-                in_=words_t[:].rearrange("p u r -> p r u"),
+                in_=words_t.rearrange("p u r -> p r u"),
             )
+
+        def new_words():
+            return psum_words.tile([P, DIM], F32, name="words")
+
+        def new_acc():
+            return psum_acc.tile([P, ROWS], F32, name="acc")
+
+        def new_back():
+            return psum_back.tile([P, DIM], F32, name="back")
 
         def new_grouped():
             return stage.tile([P, ROWS * 4], BF16, name="grouped", align_bytes=64)
 
-        def transpose_words(raw):
-            grouped = new_grouped()
-            transpose_half(raw, grouped, 0, nc.vector.tensor_copy)
-            transpose_half(raw, grouped, 1, nc.scalar.copy)
-            return grouped
-
-        def quantise(grouped, codes, scales):
+        def quantise(grouped, codes, scales, first=0, last=ROWS):
             nc.vector.quantize_mx(
-                out=codes[:].bitcast(FP8X4), scales=scales[:], in_=grouped[:]
+                out=codes[:, first:last].bitcast(FP8X4),
+                scales=scales[:, first:last],
+                in_=grouped[:, 4 * first : 4 * last],
             )
 
         def new_projected():
             return stage.tile([P, SUBS, ROWS], F32, name="projected")
 
-        def project(g, name, projected, m):
-            bias = FIRST_BIAS[name] + m
-            acc = psum_acc.tile([P, ROWS], F32, name="acc")
+        def project(g, name, projected, m, first=0, last=ROWS, new_bank=new_acc, on_vector=False):
+            bias = bias_cols[:, FIRST_BIAS[name] + m : FIRST_BIAS[name] + m + 1]
+            acc = new_bank()
             nc.tensor.matmul_mx(
-                out=acc[:],
+                out=acc[:, 0 : last - first],
                 lhsT=w_codes[name][:, m * P : (m + 1) * P].bitcast(FP8X4),
                 lhsT_scale=w_scales[name][:, m * P : (m + 1) * P],
-                rhs=x_codes[g][:].bitcast(FP8X4),
-                rhs_scale=x_scales[g][:],
+                rhs=x_codes[g][:, first:last].bitcast(FP8X4),
+                rhs_scale=x_scales[g][:, first:last],
                 start=True,
                 stop=True,
             )
-            nc.scalar.activation(
-                out=projected[:, m, :],
-                in_=acc[:],
-                func=IDENTITY,
-                bias=bias_cols[:, bias : bias + 1],
-                scale=1.0,
-            )
+            if on_vector:
+                nc.vector.tensor_scalar_add(
+                    out=projected[:, m, first:last], in0=acc[:, 0 : last - first], scalar1=bias
+                )
+            else:
+                nc.scalar.activation(
+                    out=projected[:, m, first:last],
+                    in_=acc[:, 0 : last - first],
+                    func=IDENTITY,
+                    bias=bias,
+                    scale=1.0,
+                )
 
-        def rotate(name, projected, rotated, i):
-            back = psum_back.tile([P, DIM], F32, name="back", tag="back")
+        def rotate(name, projected, rotated, i, gpsimd_sub=GPSIMD_SUB):
+            back = new_back()
             for m in range(SUBS):
                 nc.tensor.transpose(
                     back[:, m * P : (m + 1) * P],
                     projected[:, m, i * P : (i + 1) * P],
                     ident[:],
                 )
-            planes = rot_table[:, FIRST_PLANE[name] : FIRST_PLANE[name] + 2, i, :]
-            if i == GPSIMD_SUB:
+            planes = rot_table[:, FIRST_PLANE[name] : FIRST_PLANE[name] + 2, i % PAIR, :]
+            if i == gpsimd_sub:
                 back_sb = stage.tile([P, DIM], F32, name="back_sb")
                 nc.scalar.copy(out=back_sb[:], in_=back[:])
                 nc.gpsimd.tensor_tensor(
@@ -183,87 +190,136 @@ def tile_retention_pa_t_kernel(
                     op=MULT,
                 )
 
-        def store(g, name, rotated, first, last):
+        pair_outs = {"q": (out_rows[1], out_rows[0]), "k": (out_rows[2], out_rows[3])}
+
+        def store(g, name, rotated, b):
             for slot in range(2):
                 nc.sync.dma_start(
-                    out=pair_outs[name][slot][g][:, first * DIM : last * DIM],
-                    in_=rotated[:, slot, first:last, :].rearrange("p i c -> p (i c)"),
+                    out=entry_of(pair_outs[name][slot], g, b),
+                    in_=rotated[:, slot, b * PAIR : (b + 1) * PAIR, :].rearrange(
+                        "p s c -> p (s c)"
+                    ),
                 )
-
-        def spread_rotation(i):
-            spread = psum_back.tile([P, 2, DIM], BF16, name="spread", tag="back")
-            for plane in range(2):
-                nc.tensor.matmul(
-                    spread[:, plane, :],
-                    lhsT=pick[:, i // PAIR, :],
-                    rhs=rot_raw[:, plane, i % PAIR, :],
-                    start=True,
-                    stop=True,
-                )
-            nc.vector.tensor_copy(out=rot_table[:, 0:2, i, :], in_=spread[:])
-
-        pair_outs = {"q": (outs[1], outs[0]), "k": (outs[2], outs[3])}
 
         w_codes = {}
         w_scales = {}
         for name in ("q", "k"):
             w_codes[name] = keep.tile([P, ROWS], U32, name="w_codes_" + name, align_bytes=64)
             w_scales[name] = keep.tile([P, ROWS], U8, name="w_scales_" + name, align_bytes=64)
-
         x_codes = {}
         x_scales = {}
+        grouped_x = {}
 
-        def quantise_tokens(g, grouped):
+        def new_token_codes(g):
             x_codes[g] = stage.tile([P, ROWS], U32, name="x_codes", align_bytes=64)
             x_scales[g] = stage.tile([P, ROWS], U8, name="x_scales", align_bytes=64)
-            quantise(grouped, x_codes[g], x_scales[g])
 
-        grouped_wq = transpose_words(w_raw["q"])
-        grouped_x = {0: transpose_words(x_raw[0])}
+        def quantise_tokens(g):
+            new_token_codes(g)
+            quantise(grouped_x[g], x_codes[g], x_scales[g])
 
+        def transpose_tokens(g, half, copy_out, new_bank=new_words, clock=0):
+            if half == 0:
+                grouped_x[g] = new_grouped()
+            transpose_half(x_raw[g], grouped_x[g], half, copy_out, new_bank, clock)
+
+        grouped_wq = new_grouped()
+        transpose_half(w_raw["q"], grouped_wq, 0, nc.vector.tensor_copy, new_words, 5)
+        transpose_half(w_raw["q"], grouped_wq, 1, nc.scalar.copy, new_words, 1)
+        transpose_tokens(0, 0, nc.scalar.copy, new_back, 1)
         bias_rows_f32 = keep.tile([P, P], F32)
         nc.vector.tensor_copy(out=bias_rows_f32[:], in_=bias_rows[:])
-        bias_t = psum_words.tile([P, 2, HALF], F32, name="words_t")
-        nc.tensor.transpose(bias_t[:, 0, 0:P], bias_rows_f32[:], ident[:])
+        bias_t = new_words()
+        nc.tensor.transpose(bias_t[:, 0:P], bias_rows_f32[:], ident[:])
         quantise(grouped_wq, w_codes["q"], w_scales["q"])
         bias_cols = keep.tile([P, 2 * SUBS], F32)
-        nc.vector.tensor_copy(out=bias_cols[:], in_=bias_t[:, 0, 0 : 2 * SUBS])
-        quantise_tokens(0, grouped_x[0])
-        spread_rotation(0)
-        spread_rotation(1)
+        nc.vector.tensor_copy(out=bias_cols[:], in_=bias_t[:, 0 : 2 * SUBS])
+        transpose_tokens(0, 1, nc.scalar.copy, new_back, 1)
+        new_token_codes(0)
+        quantise(grouped_x[0], x_codes[0], x_scales[0], 0, HALF)
 
-        grouped_wk = transpose_words(w_raw["k"])
         projected = new_projected()
-        for m in range(SUBS):
-            project(0, "q", projected, m)
-        spread_rotation(2)
-        spread_rotation(3)
+        rotated = results.tile([P, 2, SUBS, DIM], F32, name="rotated")
+
+        def project_half(first, vector_share):
+            for m in range(SUBS):
+                project(
+                    0,
+                    "q",
+                    projected,
+                    m,
+                    first,
+                    first + HALF,
+                    new_acc if m < 2 else new_back,
+                    on_vector=m in vector_share,
+                )
+
+        project_half(0, (1, 3))
+        quantise(grouped_x[0], x_codes[0], x_scales[0], HALF, ROWS)
+        grouped_wk = new_grouped()
+        transpose_half(w_raw["k"], grouped_wk, 0, nc.scalar.copy, new_words, 1)
+        rotate("q", projected, rotated, 0, None)
+        rotate("q", projected, rotated, 1, None)
+        store(0, "q", rotated, 0)
+        transpose_half(w_raw["k"], grouped_wk, 1, nc.scalar.copy, new_words, 1)
+        project_half(HALF, ())
         quantise(grouped_wk, w_codes["k"], w_scales["k"])
-        grouped_x[1] = transpose_words(x_raw[1])
         nc.vector.tensor_scalar_mul(
             out=rot_table[:, 2, :, :], in0=rot_table[:, 0, :, :], scalar1=-1.0
         )
+        transpose_tokens(1, 0, nc.vector.tensor_copy, new_words, 1)
+        rotate("q", projected, rotated, 3)
+        rotate("q", projected, rotated, 2)
+        store(0, "q", rotated, 1)
+        transpose_tokens(1, 1, nc.vector.tensor_copy, new_words, 1)
+        next_projected = new_projected()
+        for m in range(SUBS):
+            project(0, "k", next_projected, m, 0, ROWS, new_acc if m < 2 else new_back)
+        quantise_tokens(1)
 
         steps = [(g, name) for g in range(GROUPS) for name in ("q", "k")]
-        for step, (g, name) in enumerate(steps):
-            if name == "q" and g + 1 < GROUPS:
-                quantise_tokens(g + 1, grouped_x[g + 1])
-            rotated = results.tile([P, 2, SUBS, DIM], F32, name="rotated")
-            next_projected = new_projected()
-            for first in (0, 2):
-                for m in (first, first + 1):
-                    if step + 1 < len(steps):
-                        project(steps[step + 1][0], steps[step + 1][1], next_projected, m)
-                for i in (first, first + 1):
-                    rotate(name, projected, rotated, i)
-                    if g == 0:
-                        store(g, name, rotated, i, i + 1)
-            if g > 0:
-                store(g, name, rotated, 0, SUBS)
-            if g + 2 < GROUPS:
-                if name == "q":
-                    grouped_x[g + 2] = new_grouped()
-                transpose_half(
-                    x_raw[g + 2], grouped_x[g + 2], 0 if name == "q" else 1, nc.scalar.copy
-                )
+
+        def turn(step, pair):
+            g, name = steps[step]
+            for i in BLOCK_PAIRS[pair]:
+                rotate(name, projected, rotated, i)
+
+        def passes(step, pair):
+            if step + 1 < len(steps):
+                g, name = steps[step + 1]
+                for m in (2 * pair, 2 * pair + 1):
+                    project(g, name, next_projected, m)
+
+        def ahead(step):
+            g, half = 2 + (step - 1) // 2, (step - 1) % 2
+            if g < GROUPS:
+                transpose_tokens(g, half, nc.scalar.copy)
+
+        for step in range(1, len(steps)):
+            g, name = steps[step]
             projected = next_projected
+            next_projected = new_projected()
+            rotated = results.tile([P, 2, SUBS, DIM], F32, name="rotated")
+            if step == 1:
+                turn(step, 0)
+                turn(step, 1)
+                passes(step, 0)
+                passes(step, 1)
+                ahead(step)
+            elif step == 2:
+                turn(step, 0)
+                passes(step, 0)
+                ahead(step)
+                turn(step, 1)
+                quantise_tokens(2)
+                passes(step, 1)
+            else:
+                ahead(step)
+                passes(step, 0)
+                turn(step, 0)
+                if step % 2 == 0 and 1 + step // 2 < GROUPS:
+                    quantise_tokens(1 + step // 2)
+                passes(step, 1)
+                turn(step, 1)
+            for b in range(2):
+                store(g, name, rotated, b)

@@ -290,36 +290,26 @@ def tile_retention_pa_t_kernel(
                 for m in (2 * pair, 2 * pair + 1):
                     project(g, name, next_projected, m)
 
-        def ahead(step):
-            g, half = 2 + (step - 1) // 2, (step - 1) % 2
-            if g < GROUPS:
-                transpose_tokens(g, half, nc.scalar.copy)
-
         for step in range(1, len(steps)):
             g, name = steps[step]
             projected = next_projected
             next_projected = new_projected()
             rotated = results.tile([P, 2, SUBS, DIM], F32, name="rotated")
+            if name == "q" and g + 1 < GROUPS:
+                quantise_tokens(g + 1)
             if step == 1:
                 turn(step, 0)
                 turn(step, 1)
                 passes(step, 0)
                 passes(step, 1)
-                ahead(step)
-            elif step == 2:
-                turn(step, 0)
-                passes(step, 0)
-                ahead(step)
-                turn(step, 1)
-                quantise_tokens(2)
-                passes(step, 1)
+                transpose_tokens(2, 0, nc.scalar.copy)
+                transpose_tokens(2, 1, nc.scalar.copy)
             else:
-                ahead(step)
                 passes(step, 0)
                 turn(step, 0)
-                if step % 2 == 0 and 1 + step // 2 < GROUPS:
-                    quantise_tokens(1 + step // 2)
                 passes(step, 1)
                 turn(step, 1)
+                if g + 2 < GROUPS:
+                    transpose_tokens(g + 2, 0 if name == "q" else 1, nc.scalar.copy)
             for b in range(2):
                 store(g, name, rotated, b)

@@ -17,9 +17,9 @@ ROWS = P * SUBS
 HALF = ROWS // 2
 GROUPS = TOKENS // ROWS
 PAIR = 2
+PAIR_GROUPS = 3
 WORDS = DIM // 2
 GPSIMD_SUB = 3
-BLOCK_PAIRS = ((0, 3), (1, 2))
 FIRST_BIAS = {"q": 0, "k": SUBS}
 FIRST_PLANE = {"q": 0, "k": 1}
 
@@ -34,9 +34,18 @@ def tile_retention_pa_t_kernel(
     x_rows = x.rearrange("b l k -> (b l) k")
     out_rows = [o.rearrange("b l h d -> (b l) (h d)") for o in (out_0, out_1, out_2, out_3)]
 
-    def entry_of(rows, g, b):
-        first = g * ROWS + b * HALF
-        return rows[first : first + HALF, :].rearrange("(p s) c -> p (s c)", s=PAIR)
+    def blocks_a_piece(g):
+        return PAIR if g < PAIR_GROUPS else SUBS
+
+    def pieces_of(g):
+        return SUBS // blocks_a_piece(g)
+
+    def piece_of(rows, g, piece):
+        size = P * blocks_a_piece(g)
+        first = g * ROWS + piece * size
+        return rows[first : first + size, :].rearrange(
+            "(p t) c -> p (t c)", t=blocks_a_piece(g)
+        )
 
     with tc.manual_schedule(), tc.tile_pool(name="keep", bufs=1) as keep, tc.tile_pool(
         name="x_in", bufs=GROUPS
@@ -64,15 +73,16 @@ def tile_retention_pa_t_kernel(
 
         def load_weight(raw, w, first, last):
             nc.sync.dma_start(
-                out=raw[:].rearrange("p (m k) -> p m k", m=SUBS)[:, first:last, :],
-                in_=w.rearrange("(m p) k -> p m k", p=P)[:, first:last, :],
+                out=raw[:, first * DIM : last * DIM],
+                in_=w.rearrange("(p j) k -> p (j k)", j=SUBS)[:, first * DIM : last * DIM],
             )
 
         def load_tokens(g):
-            for b in range(2):
+            width = blocks_a_piece(g) * DIM
+            for piece in range(pieces_of(g)):
                 nc.sync.dma_start(
-                    out=x_raw[g][:, b * PAIR * DIM : (b + 1) * PAIR * DIM],
-                    in_=entry_of(x_rows, g, b),
+                    out=x_raw[g][:, piece * width : (piece + 1) * width],
+                    in_=piece_of(x_rows, g, piece),
                 )
 
         w_raw = {
@@ -84,38 +94,51 @@ def tile_retention_pa_t_kernel(
         load_weight(w_raw["q"], wq_w, 0, 2)
         load_weight(w_raw["q"], wq_w, 2, 4)
         load_tokens(0)
-        rot_table = keep.tile([P, 3, PAIR, DIM], BF16)
+        pair_table = keep.tile([P, 3, PAIR, DIM], BF16)
         for plane, rot in ((0, rot_im), (1, rot_re)):
             nc.sync.dma_start(
-                out=rot_table[:, plane, :, :].rearrange("p s c -> p (s c)"),
+                out=pair_table[:, plane, :, :].rearrange("p s c -> p (s c)"),
                 in_=rot.rearrange("(p t) h d -> p (t h d)", t=PAIR),
             )
         load_weight(w_raw["k"], wk_w, 0, 4)
         for g in range(1, GROUPS):
             load_tokens(g)
 
+        quad_table = keep.tile([P, 3, SUBS, DIM], BF16)
+        ident_bf16 = keep.tile([P, P], BF16)
+        nc.vector.tensor_copy(out=ident_bf16[:], in_=ident[:])
+        pick = keep.tile([P, PAIR, P], BF16)
+        nc.vector.tensor_copy(
+            out=pick[:].rearrange("p h (r q) -> p h r q", r=PAIR),
+            in_=ident_bf16[:]
+            .rearrange("p (q h) -> p h q", h=PAIR)
+            .unsqueeze(2)
+            .to_broadcast([P, PAIR, PAIR, P // PAIR]),
+        )
+
         def keep_clock(bank, count):
             for n in range(count):
                 nc.tensor.matmul(bank, lhsT=zeros[:, 0:P], rhs=zeros[:], start=True, stop=True)
 
-        def transpose_half(raw, grouped, half, copy_out, new_bank, clock=0):
-            grouped_words = grouped[:].bitcast(F32).rearrange("p (r u) -> p r u", u=2)
+        def transpose_half(raw, out_words, order, half, copy_out, new_bank, clock=0):
             raw_words = raw[:].bitcast(F32)
             bank = new_bank()
             keep_clock(bank[:], clock)
-            words_t = bank[:].rearrange("p (u r) -> p u r", u=2)
+            words_t = bank[:].rearrange("p (u j r) -> p u j r", u=2, j=2)
             for j in range(2):
                 sub = 2 * half + j
                 for u in range(2):
                     nc.tensor.transpose(
-                        words_t[:, u, j * P : (j + 1) * P],
+                        words_t[:, u, j, :],
                         raw_words[:, sub * WORDS + u : (sub + 1) * WORDS : 2],
                         ident[:],
                     )
-            copy_out(
-                out=grouped_words[:, half * HALF : (half + 1) * HALF, :],
-                in_=words_t.rearrange("p u r -> p r u"),
-            )
+            copy_out(out=out_words, in_=words_t.rearrange("p u j r -> p " + order))
+
+        def transpose_channels(raw, grouped, half, copy_out, clock):
+            words = grouped[:].bitcast(F32).rearrange("p (r j u) -> p r j u", j=SUBS, u=2)
+            words = words[:, :, 2 * half : 2 * half + 2, :]
+            transpose_half(raw, words, "r j u", half, copy_out, new_words, clock)
 
         def new_words():
             return psum_words.tile([P, DIM], F32, name="words")
@@ -164,7 +187,7 @@ def tile_retention_pa_t_kernel(
                     scale=1.0,
                 )
 
-        def rotate(name, projected, rotated, i, gpsimd_sub=GPSIMD_SUB):
+        def rotate(g, name, projected, rotated, i, on_gpsimd=False):
             back = new_back()
             for m in range(SUBS):
                 nc.tensor.transpose(
@@ -172,8 +195,9 @@ def tile_retention_pa_t_kernel(
                     projected[:, m, i * P : (i + 1) * P],
                     ident[:],
                 )
-            planes = rot_table[:, FIRST_PLANE[name] : FIRST_PLANE[name] + 2, i % PAIR, :]
-            if i == gpsimd_sub:
+            table, entry = (pair_table, i % PAIR) if g < PAIR_GROUPS else (quad_table, i)
+            planes = table[:, FIRST_PLANE[name] : FIRST_PLANE[name] + 2, entry, :]
+            if on_gpsimd:
                 back_sb = stage.tile([P, DIM], F32, name="back_sb")
                 nc.scalar.copy(out=back_sb[:], in_=back[:])
                 nc.gpsimd.tensor_tensor(
@@ -192,14 +216,30 @@ def tile_retention_pa_t_kernel(
 
         pair_outs = {"q": (out_rows[1], out_rows[0]), "k": (out_rows[2], out_rows[3])}
 
-        def store(g, name, rotated, b):
+        def store(g, name, rotated, piece):
+            size = blocks_a_piece(g)
             for slot in range(2):
                 nc.sync.dma_start(
-                    out=entry_of(pair_outs[name][slot], g, b),
-                    in_=rotated[:, slot, b * PAIR : (b + 1) * PAIR, :].rearrange(
-                        "p s c -> p (s c)"
+                    out=piece_of(pair_outs[name][slot], g, piece),
+                    in_=rotated[:, slot, piece * size : (piece + 1) * size, :].rearrange(
+                        "p t c -> p (t c)"
                     ),
                 )
+
+        def spread_rotation(i):
+            spread = psum_back.tile([P, 2, DIM], BF16, name="spread", tag="back")
+            for plane in range(2):
+                nc.tensor.matmul(
+                    spread[:, plane, :],
+                    lhsT=pick[:, i // PAIR, :],
+                    rhs=pair_table[:, plane, i % PAIR, :],
+                    start=True,
+                    stop=True,
+                )
+            nc.scalar.copy(out=quad_table[:, 0:2, i, :], in_=spread[:])
+            nc.vector.tensor_scalar_mul(
+                out=quad_table[:, 2, i, :], in0=spread[:, 0, :], scalar1=-1.0
+            )
 
         w_codes = {}
         w_scales = {}
@@ -221,11 +261,13 @@ def tile_retention_pa_t_kernel(
         def transpose_tokens(g, half, copy_out, new_bank=new_words, clock=0):
             if half == 0:
                 grouped_x[g] = new_grouped()
-            transpose_half(x_raw[g], grouped_x[g], half, copy_out, new_bank, clock)
+            words = grouped_x[g][:].bitcast(F32).rearrange("p (j r u) -> p j r u", j=SUBS, u=2)
+            words = words[:, 2 * half : 2 * half + 2, :, :]
+            transpose_half(x_raw[g], words, "j r u", half, copy_out, new_bank, clock)
 
         grouped_wq = new_grouped()
-        transpose_half(w_raw["q"], grouped_wq, 0, nc.vector.tensor_copy, new_words, 5)
-        transpose_half(w_raw["q"], grouped_wq, 1, nc.scalar.copy, new_words, 1)
+        transpose_channels(w_raw["q"], grouped_wq, 0, nc.vector.tensor_copy, 5)
+        transpose_channels(w_raw["q"], grouped_wq, 1, nc.scalar.copy, 1)
         transpose_tokens(0, 0, nc.scalar.copy, new_back, 1)
         bias_rows_f32 = keep.tile([P, P], F32)
         nc.vector.tensor_copy(out=bias_rows_f32[:], in_=bias_rows[:])
@@ -257,19 +299,19 @@ def tile_retention_pa_t_kernel(
         project_half(0, (1, 3))
         quantise(grouped_x[0], x_codes[0], x_scales[0], HALF, ROWS)
         grouped_wk = new_grouped()
-        transpose_half(w_raw["k"], grouped_wk, 0, nc.scalar.copy, new_words, 1)
-        rotate("q", projected, rotated, 0, None)
-        rotate("q", projected, rotated, 1, None)
+        transpose_channels(w_raw["k"], grouped_wk, 0, nc.scalar.copy, 1)
+        rotate(0, "q", projected, rotated, 0)
+        rotate(0, "q", projected, rotated, 1)
         store(0, "q", rotated, 0)
-        transpose_half(w_raw["k"], grouped_wk, 1, nc.scalar.copy, new_words, 1)
+        transpose_channels(w_raw["k"], grouped_wk, 1, nc.scalar.copy, 1)
         project_half(HALF, ())
         quantise(grouped_wk, w_codes["k"], w_scales["k"])
         nc.vector.tensor_scalar_mul(
-            out=rot_table[:, 2, :, :], in0=rot_table[:, 0, :, :], scalar1=-1.0
+            out=pair_table[:, 2, :, :], in0=pair_table[:, 0, :, :], scalar1=-1.0
         )
         transpose_tokens(1, 0, nc.vector.tensor_copy, new_words, 1)
-        rotate("q", projected, rotated, 3)
-        rotate("q", projected, rotated, 2)
+        rotate(0, "q", projected, rotated, 2)
+        rotate(0, "q", projected, rotated, 3)
         store(0, "q", rotated, 1)
         transpose_tokens(1, 1, nc.vector.tensor_copy, new_words, 1)
         next_projected = new_projected()
@@ -279,10 +321,10 @@ def tile_retention_pa_t_kernel(
 
         steps = [(g, name) for g in range(GROUPS) for name in ("q", "k")]
 
-        def turn(step, pair):
+        def turn(step, blocks):
             g, name = steps[step]
-            for i in BLOCK_PAIRS[pair]:
-                rotate(name, projected, rotated, i)
+            for i in blocks:
+                rotate(g, name, projected, rotated, i, i == GPSIMD_SUB)
 
         def passes(step, pair):
             if step + 1 < len(steps):
@@ -298,18 +340,19 @@ def tile_retention_pa_t_kernel(
             if name == "q" and g + 1 < GROUPS:
                 quantise_tokens(g + 1)
             if step == 1:
-                turn(step, 0)
-                turn(step, 1)
+                turn(step, (3, 0, 1, 2))
                 passes(step, 0)
                 passes(step, 1)
                 transpose_tokens(2, 0, nc.scalar.copy)
                 transpose_tokens(2, 1, nc.scalar.copy)
             else:
                 passes(step, 0)
-                turn(step, 0)
+                turn(step, (3, 0))
                 passes(step, 1)
-                turn(step, 1)
+                turn(step, (1, 2))
                 if g + 2 < GROUPS:
                     transpose_tokens(g + 2, 0 if name == "q" else 1, nc.scalar.copy)
-            for b in range(2):
-                store(g, name, rotated, b)
+            for piece in range(pieces_of(g)):
+                store(g, name, rotated, piece)
+            if 2 <= step < 2 + SUBS:
+                spread_rotation(step - 2)

import concourse.mybir as mybir
from concourse.masks import make_identity

F32 = mybir.dt.float32
BF16 = mybir.dt.bfloat16
U32 = mybir.dt.uint32
U8 = mybir.dt.uint8
FP8X4 = mybir.dt.float8_e4m3fn_x4
MULT = mybir.AluOpType.mult
IDENTITY = mybir.ActivationFunctionType.Identity

P = 128
DIM = 512
TOKENS = 16 * 256
SUBS = 4
ROWS = P * SUBS
HALF = ROWS // 2
GROUPS = TOKENS // ROWS
PAIR = 2
PAIR_GROUPS = 3
WORDS = DIM // 2
GPSIMD_SUB = 3
FIRST_BIAS = {"q": 0, "k": SUBS}
FIRST_PLANE = {"q": 0, "k": 1}

FLOPS = 2 * TOKENS * DIM * (2 * DIM)


def tile_retention_pa_t_kernel(
    tc, x, wq_w, wq_b, wk_w, wk_b, rot_re, rot_im, out_0, out_1, out_2, out_3
):
    nc = tc.nc

    x_rows = x.rearrange("b l k -> (b l) k")
    out_rows = [o.rearrange("b l h d -> (b l) (h d)") for o in (out_0, out_1, out_2, out_3)]

    def blocks_a_piece(g):
        return PAIR if g < PAIR_GROUPS else SUBS

    def pieces_of(g):
        return SUBS // blocks_a_piece(g)

    def piece_of(rows, g, piece):
        size = P * blocks_a_piece(g)
        first = g * ROWS + piece * size
        return rows[first : first + size, :].rearrange(
            "(p t) c -> p (t c)", t=blocks_a_piece(g)
        )

    with tc.manual_schedule(), tc.tile_pool(name="keep", bufs=1) as keep, tc.tile_pool(
        name="x_in", bufs=GROUPS
    ) as x_in, tc.tile_pool(name="stage", bufs=2) as stage, tc.tile_pool(
        name="results", bufs=6
    ) as results, tc.psum_pool(name="psum_words", bufs=2) as psum_words, tc.psum_pool(
        name="psum_acc", bufs=2
    ) as psum_acc, tc.psum_pool(name="psum_back", bufs=4) as psum_back:
        zeros = keep.tile([P, DIM], BF16)
        nc.vector.memset(zeros[:], 0.0)
        ident = keep.tile([P, P], F32)
        make_identity(nc, ident[:])
        bias_rows = keep.tile([P, P], BF16)
        nc.vector.memset(bias_rows[:], 0.0)
        nc.scalar.dma_start(
            out=bias_rows[0:SUBS, :], in_=wq_b.rearrange("(m c) -> m c", c=P)
        )
        nc.scalar.dma_start(
            out=bias_rows[SUBS : 2 * SUBS, :], in_=wk_b.rearrange("(m c) -> m c", c=P)
        )

        warm = keep.tile([P, 2], F32)
        nc.vector.memset(warm[:], 0.0)
        nc.scalar.activation(out=warm[:, 1:2], in_=warm[:, 0:1], func=IDENTITY)

        def load_weight(raw, w, first, last):
            nc.sync.dma_start(
                out=raw[:, first * DIM : last * DIM],
                in_=w.rearrange("(p j) k -> p (j k)", j=SUBS)[:, first * DIM : last * DIM],
            )

        def load_tokens(g):
            width = blocks_a_piece(g) * DIM
            for piece in range(pieces_of(g)):
                nc.sync.dma_start(
                    out=x_raw[g][:, piece * width : (piece + 1) * width],
                    in_=piece_of(x_rows, g, piece),
                )

        w_raw = {
            name: keep.tile([P, SUBS * DIM], BF16, name="w_raw_" + name) for name in ("q", "k")
        }
        x_raw = [
            x_in.tile([P, SUBS * DIM], BF16, name="x_raw", tag="x_raw") for g in range(GROUPS)
        ]
        load_weight(w_raw["q"], wq_w, 0, 2)
        load_weight(w_raw["q"], wq_w, 2, 4)
        load_tokens(0)
        pair_table = keep.tile([P, 3, PAIR, DIM], BF16)
        for plane, rot in ((0, rot_im), (1, rot_re)):
            nc.sync.dma_start(
                out=pair_table[:, plane, :, :].rearrange("p s c -> p (s c)"),
                in_=rot.rearrange("(p t) h d -> p (t h d)", t=PAIR),
            )
        load_weight(w_raw["k"], wk_w, 0, 4)
        for g in range(1, GROUPS):
            load_tokens(g)

        quad_table = keep.tile([P, 3, SUBS, DIM], BF16)
        ident_bf16 = keep.tile([P, P], BF16)
        nc.vector.tensor_copy(out=ident_bf16[:], in_=ident[:])
        pick = keep.tile([P, PAIR, P], BF16)
        nc.vector.tensor_copy(
            out=pick[:].rearrange("p h (r q) -> p h r q", r=PAIR),
            in_=ident_bf16[:]
            .rearrange("p (q h) -> p h q", h=PAIR)
            .unsqueeze(2)
            .to_broadcast([P, PAIR, PAIR, P // PAIR]),
        )

        def keep_clock(bank, count):
            for n in range(count):
                nc.tensor.matmul(bank, lhsT=zeros[:, 0:P], rhs=zeros[:], start=True, stop=True)

        def transpose_half(raw, out_words, order, half, copy_out, new_bank, clock=0):
            raw_words = raw[:].bitcast(F32)
            bank = new_bank()
            keep_clock(bank[:], clock)
            words_t = bank[:].rearrange("p (u j r) -> p u j r", u=2, j=2)
            for j in range(2):
                sub = 2 * half + j
                for u in range(2):
                    nc.tensor.transpose(
                        words_t[:, u, j, :],
                        raw_words[:, sub * WORDS + u : (sub + 1) * WORDS : 2],
                        ident[:],
                    )
            copy_out(out=out_words, in_=words_t.rearrange("p u j r -> p " + order))

        def transpose_channels(raw, grouped, half, copy_out, clock):
            words = grouped[:].bitcast(F32).rearrange("p (r j u) -> p r j u", j=SUBS, u=2)
            words = words[:, :, 2 * half : 2 * half + 2, :]
            transpose_half(raw, words, "r j u", half, copy_out, new_words, clock)

        def new_words():
            return psum_words.tile([P, DIM], F32, name="words")

        def new_acc():
            return psum_acc.tile([P, ROWS], F32, name="acc")

        def new_back():
            return psum_back.tile([P, DIM], F32, name="back")

        def new_grouped():
            return stage.tile([P, ROWS * 4], BF16, name="grouped", align_bytes=64)

        def quantise(grouped, codes, scales, first=0, last=ROWS):
            nc.vector.quantize_mx(
                out=codes[:, first:last].bitcast(FP8X4),
                scales=scales[:, first:last],
                in_=grouped[:, 4 * first : 4 * last],
            )

        def new_projected():
            return stage.tile([P, SUBS, ROWS], F32, name="projected")

        def project(g, name, projected, m, first=0, last=ROWS, new_bank=new_acc, on_vector=False):
            bias = bias_cols[:, FIRST_BIAS[name] + m : FIRST_BIAS[name] + m + 1]
            acc = new_bank()
            nc.tensor.matmul_mx(
                out=acc[:, 0 : last - first],
                lhsT=w_codes[name][:, m * P : (m + 1) * P].bitcast(FP8X4),
                lhsT_scale=w_scales[name][:, m * P : (m + 1) * P],
                rhs=x_codes[g][:, first:last].bitcast(FP8X4),
                rhs_scale=x_scales[g][:, first:last],
                start=True,
                stop=True,
            )
            if on_vector:
                nc.vector.tensor_scalar_add(
                    out=projected[:, m, first:last], in0=acc[:, 0 : last - first], scalar1=bias
                )
            else:
                nc.scalar.activation(
                    out=projected[:, m, first:last],
                    in_=acc[:, 0 : last - first],
                    func=IDENTITY,
                    bias=bias,
                    scale=1.0,
                )

        def rotate(g, name, projected, rotated, i, on_gpsimd=False):
            back = new_back()
            for m in range(SUBS):
                nc.tensor.transpose(
                    back[:, m * P : (m + 1) * P],
                    projected[:, m, i * P : (i + 1) * P],
                    ident[:],
                )
            table, entry = (pair_table, i % PAIR) if g < PAIR_GROUPS else (quad_table, i)
            planes = table[:, FIRST_PLANE[name] : FIRST_PLANE[name] + 2, entry, :]
            if on_gpsimd:
                back_sb = stage.tile([P, DIM], F32, name="back_sb")
                nc.scalar.copy(out=back_sb[:], in_=back[:])
                nc.gpsimd.tensor_tensor(
                    out=rotated[:, :, i, :],
                    in0=back_sb[:].unsqueeze(1).to_broadcast([P, 2, DIM]),
                    in1=planes,
                    op=MULT,
                )
            else:
                nc.vector.tensor_tensor(
                    out=rotated[:, :, i, :],
                    in0=back[:].unsqueeze(1).to_broadcast([P, 2, DIM]),
                    in1=planes,
                    op=MULT,
                )

        pair_outs = {"q": (out_rows[1], out_rows[0]), "k": (out_rows[2], out_rows[3])}

        def store(g, name, rotated, piece):
            size = blocks_a_piece(g)
            for slot in range(2):
                nc.sync.dma_start(
                    out=piece_of(pair_outs[name][slot], g, piece),
                    in_=rotated[:, slot, piece * size : (piece + 1) * size, :].rearrange(
                        "p t c -> p (t c)"
                    ),
                )

        def spread_rotation(i):
            spread = psum_back.tile([P, 2, DIM], BF16, name="spread", tag="back")
            for plane in range(2):
                nc.tensor.matmul(
                    spread[:, plane, :],
                    lhsT=pick[:, i // PAIR, :],
                    rhs=pair_table[:, plane, i % PAIR, :],
                    start=True,
                    stop=True,
                )
            nc.scalar.copy(out=quad_table[:, 0:2, i, :], in_=spread[:])
            nc.vector.tensor_scalar_mul(
                out=quad_table[:, 2, i, :], in0=spread[:, 0, :], scalar1=-1.0
            )

        w_codes = {}
        w_scales = {}
        for name in ("q", "k"):
            w_codes[name] = keep.tile([P, ROWS], U32, name="w_codes_" + name, align_bytes=64)
            w_scales[name] = keep.tile([P, ROWS], U8, name="w_scales_" + name, align_bytes=64)
        x_codes = {}
        x_scales = {}
        grouped_x = {}

        def new_token_codes(g):
            x_codes[g] = stage.tile([P, ROWS], U32, name="x_codes", align_bytes=64)
            x_scales[g] = stage.tile([P, ROWS], U8, name="x_scales", align_bytes=64)

        def quantise_tokens(g):
            new_token_codes(g)
            quantise(grouped_x[g], x_codes[g], x_scales[g])

        def transpose_tokens(g, half, copy_out, new_bank=new_words, clock=0):
            if half == 0:
                grouped_x[g] = new_grouped()
            words = grouped_x[g][:].bitcast(F32).rearrange("p (j r u) -> p j r u", j=SUBS, u=2)
            words = words[:, 2 * half : 2 * half + 2, :, :]
            transpose_half(x_raw[g], words, "j r u", half, copy_out, new_bank, clock)

        grouped_wq = new_grouped()
        transpose_channels(w_raw["q"], grouped_wq, 0, nc.vector.tensor_copy, 5)
        transpose_channels(w_raw["q"], grouped_wq, 1, nc.scalar.copy, 1)
        transpose_tokens(0, 0, nc.scalar.copy, new_back, 1)
        bias_rows_f32 = keep.tile([P, P], F32)
        nc.vector.tensor_copy(out=bias_rows_f32[:], in_=bias_rows[:])
        bias_t = new_words()
        nc.tensor.transpose(bias_t[:, 0:P], bias_rows_f32[:], ident[:])
        quantise(grouped_wq, w_codes["q"], w_scales["q"])
        bias_cols = keep.tile([P, 2 * SUBS], F32)
        nc.vector.tensor_copy(out=bias_cols[:], in_=bias_t[:, 0 : 2 * SUBS])
        transpose_tokens(0, 1, nc.scalar.copy, new_back, 1)
        new_token_codes(0)
        quantise(grouped_x[0], x_codes[0], x_scales[0], 0, HALF)

        projected = new_projected()
        rotated = results.tile([P, 2, SUBS, DIM], F32, name="rotated")

        def project_half(first, vector_share):
            for m in range(SUBS):
                project(
                    0,
                    "q",
                    projected,
                    m,
                    first,
                    first + HALF,
                    new_acc if m < 2 else new_back,
                    on_vector=m in vector_share,
                )

        project_half(0, (1, 3))
        quantise(grouped_x[0], x_codes[0], x_scales[0], HALF, ROWS)
        grouped_wk = new_grouped()
        transpose_channels(w_raw["k"], grouped_wk, 0, nc.scalar.copy, 1)
        rotate(0, "q", projected, rotated, 0)
        rotate(0, "q", projected, rotated, 1)
        store(0, "q", rotated, 0)
        transpose_channels(w_raw["k"], grouped_wk, 1, nc.scalar.copy, 1)
        project_half(HALF, ())
        quantise(grouped_wk, w_codes["k"], w_scales["k"])
        nc.vector.tensor_scalar_mul(
            out=pair_table[:, 2, :, :], in0=pair_table[:, 0, :, :], scalar1=-1.0
        )
        transpose_tokens(1, 0, nc.vector.tensor_copy, new_words, 1)
        rotate(0, "q", projected, rotated, 2)
        rotate(0, "q", projected, rotated, 3)
        store(0, "q", rotated, 1)
        transpose_tokens(1, 1, nc.vector.tensor_copy, new_words, 1)
        next_projected = new_projected()
        for m in range(SUBS):
            project(0, "k", next_projected, m, 0, ROWS, new_acc if m < 2 else new_back)
        quantise_tokens(1)

        steps = [(g, name) for g in range(GROUPS) for name in ("q", "k")]

        def turn(step, blocks):
            g, name = steps[step]
            for i in blocks:
                rotate(g, name, projected, rotated, i, i == GPSIMD_SUB)

        def passes(step, pair):
            if step + 1 < len(steps):
                g, name = steps[step + 1]
                for m in (2 * pair, 2 * pair + 1):
                    project(g, name, next_projected, m)

        for step in range(1, len(steps)):
            g, name = steps[step]
            projected = next_projected
            next_projected = new_projected()
            rotated = results.tile([P, 2, SUBS, DIM], F32, name="rotated")
            if name == "q" and g + 1 < GROUPS:
                quantise_tokens(g + 1)
            if step == 1:
                turn(step, (3, 0, 1, 2))
                passes(step, 0)
                passes(step, 1)
                transpose_tokens(2, 0, nc.scalar.copy)
                transpose_tokens(2, 1, nc.scalar.copy)
            else:
                passes(step, 0)
                turn(step, (3, 0))
                passes(step, 1)
                turn(step, (1, 2))
                if g + 2 < GROUPS:
                    transpose_tokens(g + 2, 0 if name == "q" else 1, nc.scalar.copy)
            for piece in range(pieces_of(g)):
                store(g, name, rotated, piece)
            if 2 <= step < 2 + SUBS:
                spread_rotation(step - 2)
